import numpy as np
import ml_dtypes

BF16 = ml_dtypes.bfloat16


def bf(x):
    return np.asarray(x, np.float32).astype(BF16)


def f32(x):
    return np.asarray(x, np.float32)


def f64(x):
    return np.asarray(x).astype(np.float64)


def striped(idx):
    return np.tile(idx.reshape(-1, 16).T, (8, 1))


C, D2, D4, S, N, R, K, T, B, M = 1024, 512, 256, 256, 4096, 128, 32, 32, 128, 512


def setup_inputs():
    idx = np.concatenate([np.random.permutation(S)[:R] for _ in range(K)])
    return {
        "table": f32(np.random.standard_normal((C, S))),
        "targ": f32(0.5 * np.random.standard_normal((C, B))),
        "w_poi": bf(2.0 * np.random.standard_normal((D2, M)) / np.sqrt(C)),
        "w_in": bf(2.0 * np.random.standard_normal((D4, M)) / np.sqrt(C)),
        "w_out": bf(2.0 * np.random.standard_normal((D4, M)) / np.sqrt(C)),
        "b1": f32(0.1 * np.random.standard_normal((M, 1))),
        "w2": bf(np.random.standard_normal((M, 1)) / np.sqrt(M)),
        "offs": striped(idx),
    }


def reference(table, targ, w_poi, w_in, w_out, b1, w2, offs):
    idx = offs[:16].T.reshape(-1)
    x = f64(table)[:, idx] * np.repeat(f64(targ), T, axis=1)
    pre = f64(w_poi).T @ x[:D2] + f64(w_in).T @ x[D2:D2 + D4] + f64(w_out).T @ x[D2 + D4:] + f64(b1)
    h = np.maximum(pre, 0.0)
    e = np.exp((f64(w2) * h).sum(axis=0))
    den = np.sqrt(e.reshape(B, T).sum(axis=1))
    a = e / np.repeat(den, T)
    return x * a[None, :]

@@ -1,0 +1,119 @@
+import concourse.mybir as mybir
+
+F32 = mybir.dt.float32
+BF16 = mybir.dt.bfloat16
+U16 = mybir.dt.uint16
+MULT = mybir.AluOpType.mult
+ACT = mybir.ActivationFunctionType
+
+P = 128
+C, S, N, T, M = 1024, 256, 4096, 32, 512
+CB = C // P
+MB = M // P
+PIECE = S
+CHUNK = 512
+GROUP = 1024
+
+FLOPS = 2 * C * M * N + 2 * M * N
+
+
+def tile_new4_b_kernel(tc, table, targ, w_poi, w_in, w_out, b1, w2, offs, out):
+    nc = tc.nc
+    out_blocks = out.rearrange("(b p) j -> p b j", p=P)
+    with (
+        tc.tile_pool(name="held", bufs=1) as held,
+        tc.tile_pool(name="products", bufs=5) as products,
+        tc.tile_pool(name="staged", bufs=2) as staged,
+        tc.tile_pool(name="rows", bufs=2) as rows,
+        tc.psum_pool(name="hidden_sums", bufs=6) as hidden_sums,
+        tc.psum_pool(name="score_sums", bufs=2) as score_sums,
+    ):
+        offsets = held.tile([P, N // 16], U16, name="offsets")
+        nc.sync.dma_start(offsets[:], offs)
+        targ_sb = held.tile([P, CB, N // T], F32, name="targ_sb")
+        nc.scalar.dma_start(targ_sb[:], targ.rearrange("(b p) u -> p b u", p=P))
+        windows = []
+        for cb in range(CB):
+            window = held.tile([P, S], F32, name=f"window{cb}")
+            nc.sync.dma_start(window[:], table[cb * P : (cb + 1) * P, :])
+            windows.append(window)
+
+        w1_sb = held.tile([P, CB, M], BF16, name="w1_sb")
+        nc.scalar.dma_start(w1_sb[:, 0:4, :], w_poi.rearrange("(b p) m -> p b m", p=P))
+        nc.scalar.dma_start(w1_sb[:, 4:6, :], w_in.rearrange("(b p) m -> p b m", p=P))
+        nc.scalar.dma_start(w1_sb[:, 6:8, :], w_out.rearrange("(b p) m -> p b m", p=P))
+
+        b1_sb = held.tile([P, MB], F32, name="b1_sb")
+        w2_sb = held.tile([P, MB], BF16, name="w2_sb")
+        with nc.allow_non_contiguous_dma(reason="512 single elements, once"):
+            nc.scalar.dma_start(b1_sb[:], b1.rearrange("(b p) o -> p (b o)", p=P))
+            nc.scalar.dma_start(w2_sb[:], w2.rearrange("(b p) o -> p (b o)", p=P))
+        w2_wide = held.tile([P, MB, P], BF16, name="w2_wide")
+        nc.gpsimd.tensor_copy(w2_wide[:], w2_sb[:].unsqueeze(2).to_broadcast([P, MB, P]))
+
+        for group_start in range(0, N, GROUP):
+            e = rows.tile([P, GROUP], F32, name="e")
+            xs = []
+            for start in range(group_start, group_start + GROUP, CHUNK):
+                x = products.tile([P, CB, CHUNK], F32, name="x")
+                xs.append((start, x))
+                targ_wide = staged.tile([P, CB, CHUNK], F32, name="targ_wide")
+                x_bf = staged.tile([P, CB, CHUNK], BF16, name="x_bf")
+                pre = [
+                    hidden_sums.tile([P, CHUNK], F32, name=f"pre{mb}", tag="pre") for mb in range(MB)
+                ]
+                for cb in range(CB):
+                    nc.scalar.copy(
+                        targ_wide[:, cb, :].rearrange("p (u t) -> p u t", t=T),
+                        targ_sb[:, cb, start // T : (start + CHUNK) // T]
+                        .unsqueeze(2)
+                        .to_broadcast([P, CHUNK // T, T]),
+                    )
+                    for at in range(0, CHUNK, PIECE):
+                        first = start + at
+                        nc.vector.tensor_tensor(
+                            x[:, cb, at : at + PIECE],
+                            windows[cb][:].indirect(offsets[:, first // 16 : (first + PIECE) // 16]),
+                            targ_wide[:, cb, at : at + PIECE],
+                            MULT,
+                        )
+                    nc.scalar.copy(x_bf[:, cb, :], x[:, cb, :])
+                    for mb in range(MB):
+                        nc.tensor.matmul(
+                            pre[mb][:],
+                            w1_sb[:, cb, mb * P : (mb + 1) * P],
+                            x_bf[:, cb, :],
+                            start=(cb == 0),
+                            stop=(cb == CB - 1),
+                        )
+
+                h = staged.tile([P, MB, CHUNK], BF16, name="h")
+                score = score_sums.tile([P, CHUNK], F32, name="score")
+                for mb in range(MB):
+                    nc.scalar.activation(h[:, mb, :], pre[mb][:], ACT.Relu, bias=b1_sb[:, mb : mb + 1])
+                    nc.tensor.matmul(
+                        score[:], w2_wide[:, mb, :], h[:, mb, :], start=(mb == 0), stop=(mb == MB - 1)
+                    )
+                at = start - group_start
+                nc.scalar.activation(e[:, at : at + CHUNK], score[:], ACT.Exp)
+
+            total = rows.tile([P, GROUP // T], F32, name="total")
+            nc.vector.reduce_sum(
+                total[:], e[:].rearrange("p (u t) -> p u t", t=T), axis=mybir.AxisListType.X
+            )
+            den = rows.tile([P, GROUP // T], F32, name="den")
+            nc.scalar.activation(den[:], total[:], ACT.Sqrt)
+            inv_den = rows.tile([P, GROUP // T], F32, name="inv_den")
+            nc.vector.reciprocal(inv_den[:], den[:])
+            a = rows.tile([P, GROUP], F32, name="a")
+            nc.vector.tensor_tensor(
+                a[:].rearrange("p (u t) -> p u t", t=T),
+                e[:].rearrange("p (u t) -> p u t", t=T),
+                inv_den[:].unsqueeze(2).to_broadcast([P, GROUP // T, T]),
+                MULT,
+            )
+            for start, x in xs:
+                at = start - group_start
+                for cb in range(CB):
+                    nc.vector.tensor_tensor(x[:, cb, :], x[:, cb, :], a[:, at : at + CHUNK], MULT)
+                nc.sync.dma_start(out_blocks[:, :, start : start + CHUNK], x[:])

@@ -63,7 +63,7 @@ def tile_new4_b_kernel(tc, table, targ, w_poi, w_in, w_out, b1, w2, offs, out):
                     hidden_sums.tile([P, CHUNK], F32, name=f"pre{mb}", tag="pre") for mb in range(MB)
                 ]
                 for cb in range(CB):
-                    nc.scalar.copy(
+                    nc.gpsimd.tensor_copy(
                         targ_wide[:, cb, :].rearrange("p (u t) -> p u t", t=T),
                         targ_sb[:, cb, start // T : (start + CHUNK) // T]
                         .unsqueeze(2)

@@ -12,7 +12,11 @@ CB = C // P
 MB = M // P
 PIECE = S
 CHUNK = 512
-GROUP = 1024
+CHUNKS = N // CHUNK
+PAIR = 2
+SPREAD = 4
+RB = 2
+LAG = 3
 
 FLOPS = 2 * C * M * N + 2 * M * N
 
@@ -22,16 +26,16 @@ def tile_new4_b_kernel(tc, table, targ, w_poi, w_in, w_out, b1, w2, offs, out):
     out_blocks = out.rearrange("(b p) j -> p b j", p=P)
     with (
         tc.tile_pool(name="held", bufs=1) as held,
-        tc.tile_pool(name="products", bufs=5) as products,
+        tc.tile_pool(name="products", bufs=LAG + 2) as products,
         tc.tile_pool(name="staged", bufs=2) as staged,
-        tc.tile_pool(name="rows", bufs=2) as rows,
+        tc.tile_pool(name="rows", bufs=3) as rows,
         tc.psum_pool(name="hidden_sums", bufs=6) as hidden_sums,
         tc.psum_pool(name="score_sums", bufs=2) as score_sums,
     ):
         offsets = held.tile([P, N // 16], U16, name="offsets")
         nc.sync.dma_start(offsets[:], offs)
         targ_sb = held.tile([P, CB, N // T], F32, name="targ_sb")
-        nc.scalar.dma_start(targ_sb[:], targ.rearrange("(b p) u -> p b u", p=P))
+        nc.sync.dma_start(targ_sb[:], targ.rearrange("(b p) u -> p b u", p=P))
         windows = []
         for cb in range(CB):
             window = held.tile([P, S], F32, name=f"window{cb}")
@@ -46,74 +50,104 @@ def tile_new4_b_kernel(tc, table, targ, w_poi, w_in, w_out, b1, w2, offs, out):
         b1_sb = held.tile([P, MB], F32, name="b1_sb")
         w2_sb = held.tile([P, MB], BF16, name="w2_sb")
         with nc.allow_non_contiguous_dma(reason="512 single elements, once"):
-            nc.scalar.dma_start(b1_sb[:], b1.rearrange("(b p) o -> p (b o)", p=P))
-            nc.scalar.dma_start(w2_sb[:], w2.rearrange("(b p) o -> p (b o)", p=P))
+            nc.sync.dma_start(b1_sb[:], b1.rearrange("(b p) o -> p (b o)", p=P))
+            nc.sync.dma_start(w2_sb[:], w2.rearrange("(b p) o -> p (b o)", p=P))
         w2_wide = held.tile([P, MB, P], BF16, name="w2_wide")
         nc.gpsimd.tensor_copy(w2_wide[:], w2_sb[:].unsqueeze(2).to_broadcast([P, MB, P]))
 
-        for group_start in range(0, N, GROUP):
-            e = rows.tile([P, GROUP], F32, name="e")
-            xs = []
-            for start in range(group_start, group_start + GROUP, CHUNK):
-                x = products.tile([P, CB, CHUNK], F32, name="x")
-                xs.append((start, x))
-                targ_wide = staged.tile([P, CB, CHUNK], F32, name="targ_wide")
-                x_bf = staged.tile([P, CB, CHUNK], BF16, name="x_bf")
-                pre = [
+        targ_wide, x, x_bf, pre, e, den, a = {}, {}, {}, {}, {}, {}, {}
+
+        def spread_targ(k):
+            targ_wide[k] = staged.tile([P, CB, CHUNK], F32, name="targ_wide")
+            users = slice(k * CHUNK // T, (k + 1) * CHUNK // T)
+            for cb in range(0, CB, SPREAD):
+                nc.scalar.copy(
+                    targ_wide[k][:, cb : cb + SPREAD, :].rearrange("p b (u t) -> p b u t", t=T),
+                    targ_sb[:, cb : cb + SPREAD, users].unsqueeze(3).to_broadcast([P, SPREAD, CHUNK // T, T]),
+                )
+
+        def look_up(k, rb):
+            if rb == 0:
+                x[k] = products.tile([P, CB, CHUNK], F32, name="x")
+                x_bf[k] = staged.tile([P, CB, CHUNK], BF16, name="x_bf")
+                pre[k] = [
                     hidden_sums.tile([P, CHUNK], F32, name=f"pre{mb}", tag="pre") for mb in range(MB)
                 ]
-                for cb in range(CB):
-                    nc.gpsimd.tensor_copy(
-                        targ_wide[:, cb, :].rearrange("p (u t) -> p u t", t=T),
-                        targ_sb[:, cb, start // T : (start + CHUNK) // T]
-                        .unsqueeze(2)
-                        .to_broadcast([P, CHUNK // T, T]),
+            for cb in range(rb, rb + RB):
+                for at in range(0, CHUNK, PIECE):
+                    first = k * CHUNK + at
+                    nc.vector.tensor_tensor(
+                        x[k][:, cb, at : at + PIECE],
+                        windows[cb][:].indirect(offsets[:, first // 16 : (first + PIECE) // 16]),
+                        targ_wide[k][:, cb, at : at + PIECE],
+                        MULT,
                     )
-                    for at in range(0, CHUNK, PIECE):
-                        first = start + at
-                        nc.vector.tensor_tensor(
-                            x[:, cb, at : at + PIECE],
-                            windows[cb][:].indirect(offsets[:, first // 16 : (first + PIECE) // 16]),
-                            targ_wide[:, cb, at : at + PIECE],
-                            MULT,
-                        )
-                    nc.scalar.copy(x_bf[:, cb, :], x[:, cb, :])
-                    for mb in range(MB):
-                        nc.tensor.matmul(
-                            pre[mb][:],
-                            w1_sb[:, cb, mb * P : (mb + 1) * P],
-                            x_bf[:, cb, :],
-                            start=(cb == 0),
-                            stop=(cb == CB - 1),
-                        )
-
-                h = staged.tile([P, MB, CHUNK], BF16, name="h")
-                score = score_sums.tile([P, CHUNK], F32, name="score")
+            nc.scalar.copy(x_bf[k][:, rb : rb + RB, :], x[k][:, rb : rb + RB, :])
+            for cb in range(rb, rb + RB):
                 for mb in range(MB):
-                    nc.scalar.activation(h[:, mb, :], pre[mb][:], ACT.Relu, bias=b1_sb[:, mb : mb + 1])
                     nc.tensor.matmul(
-                        score[:], w2_wide[:, mb, :], h[:, mb, :], start=(mb == 0), stop=(mb == MB - 1)
+                        pre[k][mb][:],
+                        w1_sb[:, cb, mb * P : (mb + 1) * P],
+                        x_bf[k][:, cb, :],
+                        start=(cb == 0),
+                        stop=(cb == CB - 1),
                     )
-                at = start - group_start
-                nc.scalar.activation(e[:, at : at + CHUNK], score[:], ACT.Exp)
 
-            total = rows.tile([P, GROUP // T], F32, name="total")
+        def score(k):
+            if k % PAIR == 0:
+                e[k // PAIR] = rows.tile([P, PAIR, CHUNK], F32, name="e")
+            h = staged.tile([P, MB, CHUNK], BF16, name="h")
+            scores = score_sums.tile([P, CHUNK], F32, name="scores")
+            for mb in range(MB):
+                nc.scalar.activation(h[:, mb, :], pre[k][mb][:], ACT.Relu, bias=b1_sb[:, mb : mb + 1])
+                nc.tensor.matmul(
+                    scores[:], w2_wide[:, mb, :], h[:, mb, :], start=(mb == 0), stop=(mb == MB - 1)
+                )
+            nc.scalar.activation(e[k // PAIR][:, k % PAIR, :], scores[:], ACT.Exp)
+
+        def sum_and_root(g):
+            total = rows.tile([P, PAIR * CHUNK // T], F32, name="total")
             nc.vector.reduce_sum(
-                total[:], e[:].rearrange("p (u t) -> p u t", t=T), axis=mybir.AxisListType.X
+                total[:], e[g][:].rearrange("p k (u t) -> p (k u) t", t=T), axis=mybir.AxisListType.X
             )
-            den = rows.tile([P, GROUP // T], F32, name="den")
-            nc.scalar.activation(den[:], total[:], ACT.Sqrt)
-            inv_den = rows.tile([P, GROUP // T], F32, name="inv_den")
-            nc.vector.reciprocal(inv_den[:], den[:])
-            a = rows.tile([P, GROUP], F32, name="a")
+            den[g] = rows.tile([P, PAIR * CHUNK // T], F32, name="den")
+            nc.scalar.activation(den[g][:], total[:], ACT.Sqrt)
+
+        def weights(g):
+            inv_den = rows.tile([P, PAIR * CHUNK // T], F32, name="inv_den")
+            nc.vector.reciprocal(inv_den[:], den[g][:])
+            a[g] = rows.tile([P, PAIR, CHUNK], F32, name="a")
             nc.vector.tensor_tensor(
-                a[:].rearrange("p (u t) -> p u t", t=T),
-                e[:].rearrange("p (u t) -> p u t", t=T),
-                inv_den[:].unsqueeze(2).to_broadcast([P, GROUP // T, T]),
+                a[g][:].rearrange("p k (u t) -> p (k u) t", t=T),
+                e[g][:].rearrange("p k (u t) -> p (k u) t", t=T),
+                inv_den[:].unsqueeze(2).to_broadcast([P, PAIR * CHUNK // T, T]),
                 MULT,
             )
-            for start, x in xs:
-                at = start - group_start
-                for cb in range(CB):
-                    nc.vector.tensor_tensor(x[:, cb, :], x[:, cb, :], a[:, at : at + CHUNK], MULT)
-                nc.sync.dma_start(out_blocks[:, :, start : start + CHUNK], x[:])
+
+        def weigh_and_store(k, rb):
+            nc.vector.tensor_tensor(
+                x[k][:, rb : rb + RB, :],
+                x[k][:, rb : rb + RB, :],
+                a[k // PAIR][:, k % PAIR, :].unsqueeze(1).to_broadcast([P, RB, CHUNK]),
+                MULT,
+            )
+            nc.sync.dma_start(
+                out_blocks[:, rb : rb + RB, k * CHUNK : (k + 1) * CHUNK], x[k][:, rb : rb + RB, :]
+            )
+
+        spread_targ(0)
+        for step in range(CHUNKS + LAG):
+            late = step - LAG
+            if step + 1 < CHUNKS:
+                spread_targ(step + 1)
+            if late >= 0 and late % PAIR == 0:
+                weights(late // PAIR)
+            for rb in range(0, CB, RB):
+                if step < CHUNKS:
+                    look_up(step, rb)
+                if late >= 0:
+                    weigh_and_store(late, rb)
+            if step < CHUNKS:
+                score(step)
+            if 0 < step <= CHUNKS and step % PAIR == 0:
+                sum_and_root(step // PAIR - 1)

@@ -13,10 +13,10 @@ MB = M // P
 PIECE = S
 CHUNK = 512
 CHUNKS = N // CHUNK
-PAIR = 2
-SPREAD = 4
+USERS = CHUNK // T
+GROUP = 3
 RB = 2
-LAG = 3
+LAG = 4
 
 FLOPS = 2 * C * M * N + 2 * M * N
 
@@ -35,12 +35,12 @@ def tile_new4_b_kernel(tc, table, targ, w_poi, w_in, w_out, b1, w2, offs, out):
         offsets = held.tile([P, N // 16], U16, name="offsets")
         nc.sync.dma_start(offsets[:], offs)
         targ_sb = held.tile([P, CB, N // T], F32, name="targ_sb")
-        nc.sync.dma_start(targ_sb[:], targ.rearrange("(b p) u -> p b u", p=P))
-        windows = []
-        for cb in range(CB):
-            window = held.tile([P, S], F32, name=f"window{cb}")
-            nc.sync.dma_start(window[:], table[cb * P : (cb + 1) * P, :])
-            windows.append(window)
+        targ_blocks = targ.rearrange("(b p) u -> p b u", p=P)
+        windows = [held.tile([P, S], F32, name=f"window{cb}") for cb in range(CB)]
+        for rb in range(0, CB, RB):
+            nc.sync.dma_start(targ_sb[:, rb : rb + RB, :], targ_blocks[:, rb : rb + RB, :])
+            for cb in range(rb, rb + RB):
+                nc.sync.dma_start(windows[cb][:], table[cb * P : (cb + 1) * P, :])
 
         w1_sb = held.tile([P, CB, M], BF16, name="w1_sb")
         nc.scalar.dma_start(w1_sb[:, 0:4, :], w_poi.rearrange("(b p) m -> p b m", p=P))
@@ -57,14 +57,16 @@ def tile_new4_b_kernel(tc, table, targ, w_poi, w_in, w_out, b1, w2, offs, out):
 
         targ_wide, x, x_bf, pre, e, den, a = {}, {}, {}, {}, {}, {}, {}
 
-        def spread_targ(k):
-            targ_wide[k] = staged.tile([P, CB, CHUNK], F32, name="targ_wide")
-            users = slice(k * CHUNK // T, (k + 1) * CHUNK // T)
-            for cb in range(0, CB, SPREAD):
-                nc.scalar.copy(
-                    targ_wide[k][:, cb : cb + SPREAD, :].rearrange("p b (u t) -> p b u t", t=T),
-                    targ_sb[:, cb : cb + SPREAD, users].unsqueeze(3).to_broadcast([P, SPREAD, CHUNK // T, T]),
-                )
+        def chunks_of(g):
+            return min(GROUP, CHUNKS - g * GROUP)
+
+        def spread_targ(k, rb):
+            if rb == 0:
+                targ_wide[k] = staged.tile([P, CB, CHUNK], F32, name="targ_wide")
+            nc.scalar.copy(
+                targ_wide[k][:, rb : rb + RB, :].rearrange("p b (u t) -> p b u t", t=T),
+                targ_sb[:, rb : rb + RB, k * USERS : (k + 1) * USERS].unsqueeze(3).to_broadcast([P, RB, USERS, T]),
+            )
 
         def look_up(k, rb):
             if rb == 0:
@@ -94,8 +96,6 @@ def tile_new4_b_kernel(tc, table, targ, w_poi, w_in, w_out, b1, w2, offs, out):
                     )
 
         def score(k):
-            if k % PAIR == 0:
-                e[k // PAIR] = rows.tile([P, PAIR, CHUNK], F32, name="e")
             h = staged.tile([P, MB, CHUNK], BF16, name="h")
             scores = score_sums.tile([P, CHUNK], F32, name="scores")
             for mb in range(MB):
@@ -103,24 +103,30 @@ def tile_new4_b_kernel(tc, table, targ, w_poi, w_in, w_out, b1, w2, offs, out):
                 nc.tensor.matmul(
                     scores[:], w2_wide[:, mb, :], h[:, mb, :], start=(mb == 0), stop=(mb == MB - 1)
                 )
-            nc.scalar.activation(e[k // PAIR][:, k % PAIR, :], scores[:], ACT.Exp)
+            if k % GROUP == 0:
+                e[k // GROUP] = rows.tile([P, GROUP, CHUNK], F32, name="e")
+            nc.scalar.activation(e[k // GROUP][:, k % GROUP, :], scores[:], ACT.Exp)
 
         def sum_and_root(g):
-            total = rows.tile([P, PAIR * CHUNK // T], F32, name="total")
+            n = chunks_of(g)
+            total = rows.tile([P, GROUP * USERS], F32, name="total")
             nc.vector.reduce_sum(
-                total[:], e[g][:].rearrange("p k (u t) -> p (k u) t", t=T), axis=mybir.AxisListType.X
+                total[:, : n * USERS],
+                e[g][:, :n, :].rearrange("p k (u t) -> p (k u) t", t=T),
+                axis=mybir.AxisListType.X,
             )
-            den[g] = rows.tile([P, PAIR * CHUNK // T], F32, name="den")
-            nc.scalar.activation(den[g][:], total[:], ACT.Sqrt)
+            den[g] = rows.tile([P, GROUP * USERS], F32, name="den")
+            nc.scalar.activation(den[g][:, : n * USERS], total[:, : n * USERS], ACT.Sqrt)
 
         def weights(g):
-            inv_den = rows.tile([P, PAIR * CHUNK // T], F32, name="inv_den")
-            nc.vector.reciprocal(inv_den[:], den[g][:])
-            a[g] = rows.tile([P, PAIR, CHUNK], F32, name="a")
+            n = chunks_of(g)
+            inv_den = rows.tile([P, GROUP * USERS], F32, name="inv_den")
+            nc.vector.reciprocal(inv_den[:, : n * USERS], den[g][:, : n * USERS])
+            a[g] = rows.tile([P, GROUP, CHUNK], F32, name="a")
             nc.vector.tensor_tensor(
-                a[g][:].rearrange("p k (u t) -> p (k u) t", t=T),
-                e[g][:].rearrange("p k (u t) -> p (k u) t", t=T),
-                inv_den[:].unsqueeze(2).to_broadcast([P, PAIR * CHUNK // T, T]),
+                a[g][:, :n, :].rearrange("p k (u t) -> p (k u) t", t=T),
+                e[g][:, :n, :].rearrange("p k (u t) -> p (k u) t", t=T),
+                inv_den[:, : n * USERS].unsqueeze(2).to_broadcast([P, n * USERS, T]),
                 MULT,
             )
 
@@ -128,26 +134,29 @@ def tile_new4_b_kernel(tc, table, targ, w_poi, w_in, w_out, b1, w2, offs, out):
             nc.vector.tensor_tensor(
                 x[k][:, rb : rb + RB, :],
                 x[k][:, rb : rb + RB, :],
-                a[k // PAIR][:, k % PAIR, :].unsqueeze(1).to_broadcast([P, RB, CHUNK]),
+                a[k // GROUP][:, k % GROUP, :].unsqueeze(1).to_broadcast([P, RB, CHUNK]),
                 MULT,
             )
             nc.sync.dma_start(
                 out_blocks[:, rb : rb + RB, k * CHUNK : (k + 1) * CHUNK], x[k][:, rb : rb + RB, :]
             )
 
-        spread_targ(0)
+        turns = list(range(0, CB, RB))
+        for rb in turns:
+            spread_targ(0, rb)
         for step in range(CHUNKS + LAG):
             late = step - LAG
-            if step + 1 < CHUNKS:
-                spread_targ(step + 1)
-            if late >= 0 and late % PAIR == 0:
-                weights(late // PAIR)
-            for rb in range(0, CB, RB):
+            ends_group = 1 <= step <= CHUNKS and (step % GROUP == 0 or step == CHUNKS)
+            for rb in turns:
+                if step + 1 < CHUNKS:
+                    spread_targ(step + 1, rb)
+                if 1 <= step <= CHUNKS and rb == turns[0]:
+                    score(step - 1)
                 if step < CHUNKS:
                     look_up(step, rb)
+                if ends_group and rb == turns[1]:
+                    sum_and_root((step - 1) // GROUP)
+                if ends_group and rb == turns[-1]:
+                    weights((step - 1) // GROUP)
                 if late >= 0:
                     weigh_and_store(late, rb)
-            if step < CHUNKS:
-                score(step)
-            if 0 < step <= CHUNKS and step % PAIR == 0:
-                sum_and_root(step // PAIR - 1)

@@ -1,4 +1,5 @@
 import concourse.mybir as mybir
+from concourse.masks import make_block_diagonal, make_identity
 
 F32 = mybir.dt.float32
 BF16 = mybir.dt.bfloat16
@@ -14,9 +15,10 @@ PIECE = S
 CHUNK = 512
 CHUNKS = N // CHUNK
 USERS = CHUNK // T
+JB = CHUNK // P
 GROUP = 3
 RB = 2
-LAG = 4
+LAG = 5
 
 FLOPS = 2 * C * M * N + 2 * M * N
 
@@ -28,9 +30,10 @@ def tile_new4_b_kernel(tc, table, targ, w_poi, w_in, w_out, b1, w2, offs, out):
         tc.tile_pool(name="held", bufs=1) as held,
         tc.tile_pool(name="products", bufs=LAG + 2) as products,
         tc.tile_pool(name="staged", bufs=2) as staged,
-        tc.tile_pool(name="rows", bufs=3) as rows,
-        tc.psum_pool(name="hidden_sums", bufs=6) as hidden_sums,
-        tc.psum_pool(name="score_sums", bufs=2) as score_sums,
+        tc.tile_pool(name="columns", bufs=3) as columns,
+        tc.psum_pool(name="hidden_sums", bufs=5) as hidden_sums,
+        tc.psum_pool(name="column_sums", bufs=1) as column_sums,
+        tc.psum_pool(name="weight_rows", bufs=2) as weight_rows,
     ):
         offsets = held.tile([P, N // 16], U16, name="offsets")
         nc.sync.dma_start(offsets[:], offs)
@@ -52,10 +55,14 @@ def tile_new4_b_kernel(tc, table, targ, w_poi, w_in, w_out, b1, w2, offs, out):
         with nc.allow_non_contiguous_dma(reason="512 single elements, once"):
             nc.sync.dma_start(b1_sb[:], b1.rearrange("(b p) o -> p (b o)", p=P))
             nc.sync.dma_start(w2_sb[:], w2.rearrange("(b p) o -> p (b o)", p=P))
-        w2_wide = held.tile([P, MB, P], BF16, name="w2_wide")
-        nc.gpsimd.tensor_copy(w2_wide[:], w2_sb[:].unsqueeze(2).to_broadcast([P, MB, P]))
+        same_user = held.tile([P, P], F32, name="same_user")
+        make_block_diagonal(nc, same_user[:], T)
+        identity = held.tile([P, P], F32, name="identity")
+        make_identity(nc, identity[:])
+        ones = held.tile([P, P], F32, name="ones")
+        nc.gpsimd.memset(ones[:], 1.0)
 
-        targ_wide, x, x_bf, pre, e, den, a = {}, {}, {}, {}, {}, {}, {}
+        targ_wide, x, x_bf, pre, sums, e, den, a, a_rows = {}, {}, {}, {}, {}, {}, {}, {}, {}
 
         def chunks_of(g):
             return min(GROUP, CHUNKS - g * GROUP)
@@ -96,45 +103,54 @@ def tile_new4_b_kernel(tc, table, targ, w_poi, w_in, w_out, b1, w2, offs, out):
                     )
 
         def score(k):
+            g, first = k // GROUP, (k % GROUP) * JB
+            if first == 0:
+                sums[g] = column_sums.tile([P, 2, GROUP * JB], F32, name="sums")
+                e[g] = columns.tile([P, GROUP * JB], F32, name="e")
             h = staged.tile([P, MB, CHUNK], BF16, name="h")
-            scores = score_sums.tile([P, CHUNK], F32, name="scores")
             for mb in range(MB):
                 nc.scalar.activation(h[:, mb, :], pre[k][mb][:], ACT.Relu, bias=b1_sb[:, mb : mb + 1])
-                nc.tensor.matmul(
-                    scores[:], w2_wide[:, mb, :], h[:, mb, :], start=(mb == 0), stop=(mb == MB - 1)
-                )
-            if k % GROUP == 0:
-                e[k // GROUP] = rows.tile([P, GROUP, CHUNK], F32, name="e")
-            nc.scalar.activation(e[k // GROUP][:, k % GROUP, :], scores[:], ACT.Exp)
+            for jb in range(JB):
+                for mb in range(MB):
+                    nc.tensor.matmul(
+                        sums[g][:, 0, first + jb : first + jb + 1],
+                        h[:, mb, jb * P : (jb + 1) * P],
+                        w2_sb[:, mb : mb + 1],
+                        start=(mb == 0),
+                        stop=(mb == MB - 1),
+                    )
+            nc.scalar.activation(e[g][:, first : first + JB], sums[g][:, 0, first : first + JB], ACT.Exp)
 
         def sum_and_root(g):
-            n = chunks_of(g)
-            total = rows.tile([P, GROUP * USERS], F32, name="total")
-            nc.vector.reduce_sum(
-                total[:, : n * USERS],
-                e[g][:, :n, :].rearrange("p k (u t) -> p (k u) t", t=T),
-                axis=mybir.AxisListType.X,
-            )
-            den[g] = rows.tile([P, GROUP * USERS], F32, name="den")
-            nc.scalar.activation(den[g][:, : n * USERS], total[:, : n * USERS], ACT.Sqrt)
+            n = chunks_of(g) * JB
+            nc.tensor.matmul(sums[g][:, 1, :n], same_user[:], e[g][:, :n], start=True, stop=True)
+            den[g] = columns.tile([P, GROUP * JB], F32, name="den")
+            nc.scalar.activation(den[g][:, :n], sums[g][:, 1, :n], ACT.Sqrt)
 
         def weights(g):
-            n = chunks_of(g)
-            inv_den = rows.tile([P, GROUP * USERS], F32, name="inv_den")
-            nc.vector.reciprocal(inv_den[:, : n * USERS], den[g][:, : n * USERS])
-            a[g] = rows.tile([P, GROUP, CHUNK], F32, name="a")
-            nc.vector.tensor_tensor(
-                a[g][:, :n, :].rearrange("p k (u t) -> p (k u) t", t=T),
-                e[g][:, :n, :].rearrange("p k (u t) -> p (k u) t", t=T),
-                inv_den[:, : n * USERS].unsqueeze(2).to_broadcast([P, n * USERS, T]),
-                MULT,
+            n = chunks_of(g) * JB
+            inv_den = columns.tile([P, GROUP * JB], F32, name="inv_den")
+            nc.vector.reciprocal(inv_den[:, :n], den[g][:, :n])
+            a[g] = columns.tile([P, GROUP * JB], F32, name="a")
+            nc.vector.tensor_tensor(a[g][:, :n], e[g][:, :n], inv_den[:, :n], MULT)
+
+        def spread_weights(k):
+            g, first = k // GROUP, (k % GROUP) * JB
+            diagonals = staged.tile([P, JB, P], F32, name="diagonals")
+            for jb in range(JB):
+                nc.scalar.activation(
+                    diagonals[:, jb, :], identity[:], ACT.Copy, scale=a[g][:, first + jb : first + jb + 1]
+                )
+            a_rows[k] = weight_rows.tile([P, CHUNK], F32, name="a_rows")
+            nc.tensor.matmul(
+                a_rows[k][:], ones[:], diagonals[:].rearrange("p b j -> p (b j)"), start=True, stop=True
             )
 
         def weigh_and_store(k, rb):
             nc.vector.tensor_tensor(
                 x[k][:, rb : rb + RB, :],
                 x[k][:, rb : rb + RB, :],
-                a[k // GROUP][:, k % GROUP, :].unsqueeze(1).to_broadcast([P, RB, CHUNK]),
+                a_rows[k][:].unsqueeze(1).to_broadcast([P, RB, CHUNK]),
                 MULT,
             )
             nc.sync.dma_start(
@@ -156,7 +172,9 @@ def tile_new4_b_kernel(tc, table, targ, w_poi, w_in, w_out, b1, w2, offs, out):
                     look_up(step, rb)
                 if ends_group and rb == turns[1]:
                     sum_and_root((step - 1) // GROUP)
-                if ends_group and rb == turns[-1]:
+                if ends_group and rb == turns[2]:
                     weights((step - 1) // GROUP)
+                if 0 <= late + 1 < CHUNKS and rb == turns[3]:
+                    spread_weights(late + 1)
                 if late >= 0:
                     weigh_and_store(late, rb)

@@ -91,7 +91,10 @@ def tile_new4_b_kernel(tc, table, targ, w_poi, w_in, w_out, b1, w2, offs, out):
                         targ_wide[k][:, cb, at : at + PIECE],
                         MULT,
                     )
-            nc.scalar.copy(x_bf[k][:, rb : rb + RB, :], x[k][:, rb : rb + RB, :])
+            if k < LAG and rb == CB - RB:
+                nc.vector.tensor_copy(x_bf[k][:, rb : rb + RB, :], x[k][:, rb : rb + RB, :])
+            else:
+                nc.scalar.copy(x_bf[k][:, rb : rb + RB, :], x[k][:, rb : rb + RB, :])
             for cb in range(rb, rb + RB):
                 for mb in range(MB):
                     nc.tensor.matmul(
@@ -174,7 +177,7 @@ def tile_new4_b_kernel(tc, table, targ, w_poi, w_in, w_out, b1, w2, offs, out):
                     sum_and_root((step - 1) // GROUP)
                 if ends_group and rb == turns[2]:
                     weights((step - 1) // GROUP)
-                if 0 <= late + 1 < CHUNKS and rb == turns[3]:
+                if 0 <= late + 1 < CHUNKS and rb == turns[1]:
                     spread_weights(late + 1)
                 if late >= 0:
                     weigh_and_store(late, rb)

@@ -62,7 +62,7 @@ def tile_new4_b_kernel(tc, table, targ, w_poi, w_in, w_out, b1, w2, offs, out):
         ones = held.tile([P, P], F32, name="ones")
         nc.gpsimd.memset(ones[:], 1.0)
 
-        targ_wide, x, x_bf, pre, sums, e, den, a, a_rows = {}, {}, {}, {}, {}, {}, {}, {}, {}
+        targ_wide, x, x_bf, pre, sums, e, inv_den, a, a_rows = {}, {}, {}, {}, {}, {}, {}, {}, {}
 
         def chunks_of(g):
             return min(GROUP, CHUNKS - g * GROUP)
@@ -70,10 +70,12 @@ def tile_new4_b_kernel(tc, table, targ, w_poi, w_in, w_out, b1, w2, offs, out):
         def spread_targ(k, rb):
             if rb == 0:
                 targ_wide[k] = staged.tile([P, CB, CHUNK], F32, name="targ_wide")
-            nc.scalar.copy(
-                targ_wide[k][:, rb : rb + RB, :].rearrange("p b (u t) -> p b u t", t=T),
-                targ_sb[:, rb : rb + RB, k * USERS : (k + 1) * USERS].unsqueeze(3).to_broadcast([P, RB, USERS, T]),
-            )
+            wide = targ_wide[k][:, rb : rb + RB, :].rearrange("p b (u t) -> p b u t", t=T)
+            narrow = targ_sb[:, rb : rb + RB, k * USERS : (k + 1) * USERS].unsqueeze(3)
+            if k == 0 and rb == 0:
+                nc.vector.tensor_copy(wide, narrow.to_broadcast([P, RB, USERS, T]))
+            else:
+                nc.scalar.copy(wide, narrow.to_broadcast([P, RB, USERS, T]))
 
         def look_up(k, rb):
             if rb == 0:
@@ -95,8 +97,8 @@ def tile_new4_b_kernel(tc, table, targ, w_poi, w_in, w_out, b1, w2, offs, out):
                 nc.vector.tensor_copy(x_bf[k][:, rb : rb + RB, :], x[k][:, rb : rb + RB, :])
             else:
                 nc.scalar.copy(x_bf[k][:, rb : rb + RB, :], x[k][:, rb : rb + RB, :])
-            for cb in range(rb, rb + RB):
-                for mb in range(MB):
+            for mb in range(MB):
+                for cb in range(rb, rb + RB):
                     nc.tensor.matmul(
                         pre[k][mb][:],
                         w1_sb[:, cb, mb * P : (mb + 1) * P],
@@ -127,15 +129,13 @@ def tile_new4_b_kernel(tc, table, targ, w_poi, w_in, w_out, b1, w2, offs, out):
         def sum_and_root(g):
             n = chunks_of(g) * JB
             nc.tensor.matmul(sums[g][:, 1, :n], same_user[:], e[g][:, :n], start=True, stop=True)
-            den[g] = columns.tile([P, GROUP * JB], F32, name="den")
-            nc.scalar.activation(den[g][:, :n], sums[g][:, 1, :n], ACT.Sqrt)
+            inv_den[g] = columns.tile([P, GROUP * JB], F32, name="inv_den")
+            nc.scalar.activation(inv_den[g][:, :n], sums[g][:, 1, :n], ACT.Abs_reciprocal_sqrt)
 
         def weights(g):
             n = chunks_of(g) * JB
-            inv_den = columns.tile([P, GROUP * JB], F32, name="inv_den")
-            nc.vector.reciprocal(inv_den[:, :n], den[g][:, :n])
             a[g] = columns.tile([P, GROUP * JB], F32, name="a")
-            nc.vector.tensor_tensor(a[g][:, :n], e[g][:, :n], inv_den[:, :n], MULT)
+            nc.vector.tensor_tensor(a[g][:, :n], e[g][:, :n], inv_den[g][:, :n], MULT)
 
         def spread_weights(k):
             g, first = k // GROUP, (k % GROUP) * JB
@@ -149,15 +149,15 @@ def tile_new4_b_kernel(tc, table, targ, w_poi, w_in, w_out, b1, w2, offs, out):
                 a_rows[k][:], ones[:], diagonals[:].rearrange("p b j -> p (b j)"), start=True, stop=True
             )
 
-        def weigh_and_store(k, rb):
+        def weigh_and_store(k, cb, blocks):
             nc.vector.tensor_tensor(
-                x[k][:, rb : rb + RB, :],
-                x[k][:, rb : rb + RB, :],
-                a_rows[k][:].unsqueeze(1).to_broadcast([P, RB, CHUNK]),
+                x[k][:, cb : cb + blocks, :],
+                x[k][:, cb : cb + blocks, :],
+                a_rows[k][:].unsqueeze(1).to_broadcast([P, blocks, CHUNK]),
                 MULT,
             )
             nc.sync.dma_start(
-                out_blocks[:, rb : rb + RB, k * CHUNK : (k + 1) * CHUNK], x[k][:, rb : rb + RB, :]
+                out_blocks[:, cb : cb + blocks, k * CHUNK : (k + 1) * CHUNK], x[k][:, cb : cb + blocks, :]
             )
 
         turns = list(range(0, CB, RB))
@@ -179,5 +179,8 @@ def tile_new4_b_kernel(tc, table, targ, w_poi, w_in, w_out, b1, w2, offs, out):
                     weights((step - 1) // GROUP)
                 if 0 <= late + 1 < CHUNKS and rb == turns[1]:
                     spread_weights(late + 1)
-                if late >= 0:
-                    weigh_and_store(late, rb)
+                if late == CHUNKS - 1 and rb == turns[-1]:
+                    for cb in range(rb, rb + RB):
+                        weigh_and_store(late, cb, 1)
+                elif late >= 0:
+                    weigh_and_store(late, rb, RB)

@@ -19,6 +19,8 @@ JB = CHUNK // P
 GROUP = 3
 RB = 2
 LAG = 5
+GP_COLS = P
+V_COLS = CHUNK - GP_COLS
 
 FLOPS = 2 * C * M * N + 2 * M * N
 
@@ -31,6 +33,7 @@ def tile_new4_b_kernel(tc, table, targ, w_poi, w_in, w_out, b1, w2, offs, out):
         tc.tile_pool(name="products", bufs=LAG + 2) as products,
         tc.tile_pool(name="staged", bufs=2) as staged,
         tc.tile_pool(name="columns", bufs=3) as columns,
+        tc.tile_pool(name="rows", bufs=2) as rows,
         tc.psum_pool(name="hidden_sums", bufs=5) as hidden_sums,
         tc.psum_pool(name="column_sums", bufs=1) as column_sums,
         tc.psum_pool(name="weight_rows", bufs=2) as weight_rows,
@@ -149,16 +152,30 @@ def tile_new4_b_kernel(tc, table, targ, w_poi, w_in, w_out, b1, w2, offs, out):
                 a_rows[k][:], ones[:], diagonals[:].rearrange("p b j -> p (b j)"), start=True, stop=True
             )
 
-        def weigh_and_store(k, cb, blocks):
-            nc.vector.tensor_tensor(
-                x[k][:, cb : cb + blocks, :],
-                x[k][:, cb : cb + blocks, :],
-                a_rows[k][:].unsqueeze(1).to_broadcast([P, blocks, CHUNK]),
+        def weigh_and_store(k):
+            gp_row = rows.tile([P, GP_COLS], F32, name="gp_row")
+            nc.vector.tensor_copy(gp_row[:], a_rows[k][:, V_COLS:])
+            nc.gpsimd.tensor_tensor(
+                x[k][:, :, V_COLS:],
+                x[k][:, :, V_COLS:],
+                gp_row[:].unsqueeze(1).to_broadcast([P, CB, GP_COLS]),
                 MULT,
             )
-            nc.sync.dma_start(
-                out_blocks[:, cb : cb + blocks, k * CHUNK : (k + 1) * CHUNK], x[k][:, cb : cb + blocks, :]
-            )
+            pieces = [(cb, RB) for cb in range(0, CB, RB)]
+            if k == CHUNKS - 1:
+                pieces = pieces[:-1] + [(cb, 1) for cb in range(CB - RB, CB)]
+            first = k * CHUNK
+            for cb, blocks in pieces:
+                nc.vector.tensor_tensor(
+                    x[k][:, cb : cb + blocks, :V_COLS],
+                    x[k][:, cb : cb + blocks, :V_COLS],
+                    a_rows[k][:, :V_COLS].unsqueeze(1).to_broadcast([P, blocks, V_COLS]),
+                    MULT,
+                )
+                nc.sync.dma_start(
+                    out_blocks[:, cb : cb + blocks, first : first + V_COLS], x[k][:, cb : cb + blocks, :V_COLS]
+                )
+            nc.sync.dma_start(out_blocks[:, :, first + V_COLS : first + CHUNK], x[k][:, :, V_COLS:])
 
         turns = list(range(0, CB, RB))
         for rb in turns:
@@ -179,8 +196,5 @@ def tile_new4_b_kernel(tc, table, targ, w_poi, w_in, w_out, b1, w2, offs, out):
                     weights((step - 1) // GROUP)
                 if 0 <= late + 1 < CHUNKS and rb == turns[1]:
                     spread_weights(late + 1)
-                if late == CHUNKS - 1 and rb == turns[-1]:
-                    for cb in range(rb, rb + RB):
-                        weigh_and_store(late, cb, 1)
-                elif late >= 0:
-                    weigh_and_store(late, rb, RB)
+            if late >= 0:
+                weigh_and_store(late)

@@ -34,6 +34,7 @@ def tile_new4_b_kernel(tc, table, targ, w_poi, w_in, w_out, b1, w2, offs, out):
         tc.tile_pool(name="staged", bufs=2) as staged,
         tc.tile_pool(name="columns", bufs=3) as columns,
         tc.tile_pool(name="rows", bufs=2) as rows,
+        tc.tile_pool(name="outgoing", bufs=8) as outgoing,
         tc.psum_pool(name="hidden_sums", bufs=5) as hidden_sums,
         tc.psum_pool(name="column_sums", bufs=1) as column_sums,
         tc.psum_pool(name="weight_rows", bufs=2) as weight_rows,
@@ -155,27 +156,26 @@ def tile_new4_b_kernel(tc, table, targ, w_poi, w_in, w_out, b1, w2, offs, out):
         def weigh_and_store(k):
             gp_row = rows.tile([P, GP_COLS], F32, name="gp_row")
             nc.vector.tensor_copy(gp_row[:], a_rows[k][:, V_COLS:])
-            nc.gpsimd.tensor_tensor(
-                x[k][:, :, V_COLS:],
-                x[k][:, :, V_COLS:],
-                gp_row[:].unsqueeze(1).to_broadcast([P, CB, GP_COLS]),
-                MULT,
-            )
             pieces = [(cb, RB) for cb in range(0, CB, RB)]
             if k == CHUNKS - 1:
                 pieces = pieces[:-1] + [(cb, 1) for cb in range(CB - RB, CB)]
-            first = k * CHUNK
             for cb, blocks in pieces:
+                weighted = outgoing.tile([P, RB, CHUNK], F32, name="weighted")
+                nc.gpsimd.tensor_tensor(
+                    weighted[:, :blocks, V_COLS:],
+                    x[k][:, cb : cb + blocks, V_COLS:],
+                    gp_row[:].unsqueeze(1).to_broadcast([P, blocks, GP_COLS]),
+                    MULT,
+                )
                 nc.vector.tensor_tensor(
-                    x[k][:, cb : cb + blocks, :V_COLS],
+                    weighted[:, :blocks, :V_COLS],
                     x[k][:, cb : cb + blocks, :V_COLS],
                     a_rows[k][:, :V_COLS].unsqueeze(1).to_broadcast([P, blocks, V_COLS]),
                     MULT,
                 )
                 nc.sync.dma_start(
-                    out_blocks[:, cb : cb + blocks, first : first + V_COLS], x[k][:, cb : cb + blocks, :V_COLS]
+                    out_blocks[:, cb : cb + blocks, k * CHUNK : (k + 1) * CHUNK], weighted[:, :blocks, :]
                 )
-            nc.sync.dma_start(out_blocks[:, :, first + V_COLS : first + CHUNK], x[k][:, :, V_COLS:])
 
         turns = list(range(0, CB, RB))
         for rb in turns:
@@ -196,5 +196,5 @@ def tile_new4_b_kernel(tc, table, targ, w_poi, w_in, w_out, b1, w2, offs, out):
                     weights((step - 1) // GROUP)
                 if 0 <= late + 1 < CHUNKS and rb == turns[1]:
                     spread_weights(late + 1)
-            if late >= 0:
-                weigh_and_store(late)
+                if late >= 0 and rb == turns[1]:
+                    weigh_and_store(late)

@@ -30,11 +30,11 @@ def tile_new4_b_kernel(tc, table, targ, w_poi, w_in, w_out, b1, w2, offs, out):
     out_blocks = out.rearrange("(b p) j -> p b j", p=P)
     with (
         tc.tile_pool(name="held", bufs=1) as held,
-        tc.tile_pool(name="products", bufs=LAG + 2) as products,
+        tc.tile_pool(name="products", bufs=LAG + 1) as products,
         tc.tile_pool(name="staged", bufs=2) as staged,
         tc.tile_pool(name="columns", bufs=3) as columns,
         tc.tile_pool(name="rows", bufs=2) as rows,
-        tc.tile_pool(name="outgoing", bufs=8) as outgoing,
+        tc.tile_pool(name="outgoing", bufs=6) as outgoing,
         tc.psum_pool(name="hidden_sums", bufs=5) as hidden_sums,
         tc.psum_pool(name="column_sums", bufs=1) as column_sums,
         tc.psum_pool(name="weight_rows", bufs=2) as weight_rows,
@@ -156,11 +156,12 @@ def tile_new4_b_kernel(tc, table, targ, w_poi, w_in, w_out, b1, w2, offs, out):
         def weigh_and_store(k):
             gp_row = rows.tile([P, GP_COLS], F32, name="gp_row")
             nc.vector.tensor_copy(gp_row[:], a_rows[k][:, V_COLS:])
-            pieces = [(cb, RB) for cb in range(0, CB, RB)]
+            per = RB if k + LAG < CHUNKS else 2 * RB
+            pieces = [(cb, per) for cb in range(0, CB, per)]
             if k == CHUNKS - 1:
-                pieces = pieces[:-1] + [(cb, 1) for cb in range(CB - RB, CB)]
+                pieces = pieces[:-1] + [(CB - 2 * RB, RB)] + [(cb, 1) for cb in range(CB - RB, CB)]
             for cb, blocks in pieces:
-                weighted = outgoing.tile([P, RB, CHUNK], F32, name="weighted")
+                weighted = outgoing.tile([P, 2 * RB, CHUNK], F32, name="weighted")
                 nc.gpsimd.tensor_tensor(
                     weighted[:, :blocks, V_COLS:],
                     x[k][:, cb : cb + blocks, V_COLS:],

import concourse.mybir as mybir
from concourse.masks import make_block_diagonal, make_identity

F32 = mybir.dt.float32
BF16 = mybir.dt.bfloat16
U16 = mybir.dt.uint16
MULT = mybir.AluOpType.mult
ACT = mybir.ActivationFunctionType

P = 128
C, S, N, T, M = 1024, 256, 4096, 32, 512
CB = C // P
MB = M // P
PIECE = S
CHUNK = 512
CHUNKS = N // CHUNK
USERS = CHUNK // T
JB = CHUNK // P
GROUP = 3
RB = 2
LAG = 5
GP_COLS = P
V_COLS = CHUNK - GP_COLS

FLOPS = 2 * C * M * N + 2 * M * N


def tile_new4_b_kernel(tc, table, targ, w_poi, w_in, w_out, b1, w2, offs, out):
    nc = tc.nc
    out_blocks = out.rearrange("(b p) j -> p b j", p=P)
    with (
        tc.tile_pool(name="held", bufs=1) as held,
        tc.tile_pool(name="products", bufs=LAG + 1) as products,
        tc.tile_pool(name="staged", bufs=2) as staged,
        tc.tile_pool(name="columns", bufs=3) as columns,
        tc.tile_pool(name="rows", bufs=2) as rows,
        tc.tile_pool(name="outgoing", bufs=6) as outgoing,
        tc.psum_pool(name="hidden_sums", bufs=5) as hidden_sums,
        tc.psum_pool(name="column_sums", bufs=1) as column_sums,
        tc.psum_pool(name="weight_rows", bufs=2) as weight_rows,
    ):
        offsets = held.tile([P, N // 16], U16, name="offsets")
        nc.sync.dma_start(offsets[:], offs)
        targ_sb = held.tile([P, CB, N // T], F32, name="targ_sb")
        targ_blocks = targ.rearrange("(b p) u -> p b u", p=P)
        windows = [held.tile([P, S], F32, name=f"window{cb}") for cb in range(CB)]
        for rb in range(0, CB, RB):
            nc.sync.dma_start(targ_sb[:, rb : rb + RB, :], targ_blocks[:, rb : rb + RB, :])
            for cb in range(rb, rb + RB):
                nc.sync.dma_start(windows[cb][:], table[cb * P : (cb + 1) * P, :])

        w1_sb = held.tile([P, CB, M], BF16, name="w1_sb")
        nc.scalar.dma_start(w1_sb[:, 0:4, :], w_poi.rearrange("(b p) m -> p b m", p=P))
        nc.scalar.dma_start(w1_sb[:, 4:6, :], w_in.rearrange("(b p) m -> p b m", p=P))
        nc.scalar.dma_start(w1_sb[:, 6:8, :], w_out.rearrange("(b p) m -> p b m", p=P))

        b1_sb = held.tile([P, MB], F32, name="b1_sb")
        w2_sb = held.tile([P, MB], BF16, name="w2_sb")
        with nc.allow_non_contiguous_dma(reason="512 single elements, once"):
            nc.sync.dma_start(b1_sb[:], b1.rearrange("(b p) o -> p (b o)", p=P))
            nc.sync.dma_start(w2_sb[:], w2.rearrange("(b p) o -> p (b o)", p=P))
        same_user = held.tile([P, P], F32, name="same_user")
        make_block_diagonal(nc, same_user[:], T)
        identity = held.tile([P, P], F32, name="identity")
        make_identity(nc, identity[:])
        ones = held.tile([P, P], F32, name="ones")
        nc.gpsimd.memset(ones[:], 1.0)

        targ_wide, x, x_bf, pre, sums, e, inv_den, a, a_rows = {}, {}, {}, {}, {}, {}, {}, {}, {}

        def chunks_of(g):
            return min(GROUP, CHUNKS - g * GROUP)

        def spread_targ(k, rb):
            if rb == 0:
                targ_wide[k] = staged.tile([P, CB, CHUNK], F32, name="targ_wide")
            wide = targ_wide[k][:, rb : rb + RB, :].rearrange("p b (u t) -> p b u t", t=T)
            narrow = targ_sb[:, rb : rb + RB, k * USERS : (k + 1) * USERS].unsqueeze(3)
            if k == 0 and rb == 0:
                nc.vector.tensor_copy(wide, narrow.to_broadcast([P, RB, USERS, T]))
            else:
                nc.scalar.copy(wide, narrow.to_broadcast([P, RB, USERS, T]))

        def look_up(k, rb):
            if rb == 0:
                x[k] = products.tile([P, CB, CHUNK], F32, name="x")
                x_bf[k] = staged.tile([P, CB, CHUNK], BF16, name="x_bf")
                pre[k] = [
                    hidden_sums.tile([P, CHUNK], F32, name=f"pre{mb}", tag="pre") for mb in range(MB)
                ]
            for cb in range(rb, rb + RB):
                for at in range(0, CHUNK, PIECE):
                    first = k * CHUNK + at
                    nc.vector.tensor_tensor(
                        x[k][:, cb, at : at + PIECE],
                        windows[cb][:].indirect(offsets[:, first // 16 : (first + PIECE) // 16]),
                        targ_wide[k][:, cb, at : at + PIECE],
                        MULT,
                    )
            if k < LAG and rb == CB - RB:
                nc.vector.tensor_copy(x_bf[k][:, rb : rb + RB, :], x[k][:, rb : rb + RB, :])
            else:
                nc.scalar.copy(x_bf[k][:, rb : rb + RB, :], x[k][:, rb : rb + RB, :])
            for mb in range(MB):
                for cb in range(rb, rb + RB):
                    nc.tensor.matmul(
                        pre[k][mb][:],
                        w1_sb[:, cb, mb * P : (mb + 1) * P],
                        x_bf[k][:, cb, :],
                        start=(cb == 0),
                        stop=(cb == CB - 1),
                    )

        def score(k):
            g, first = k // GROUP, (k % GROUP) * JB
            if first == 0:
                sums[g] = column_sums.tile([P, 2, GROUP * JB], F32, name="sums")
                e[g] = columns.tile([P, GROUP * JB], F32, name="e")
            h = staged.tile([P, MB, CHUNK], BF16, name="h")
            for mb in range(MB):
                nc.scalar.activation(h[:, mb, :], pre[k][mb][:], ACT.Relu, bias=b1_sb[:, mb : mb + 1])
            for jb in range(JB):
                for mb in range(MB):
                    nc.tensor.matmul(
                        sums[g][:, 0, first + jb : first + jb + 1],
                        h[:, mb, jb * P : (jb + 1) * P],
                        w2_sb[:, mb : mb + 1],
                        start=(mb == 0),
                        stop=(mb == MB - 1),
                    )
            nc.scalar.activation(e[g][:, first : first + JB], sums[g][:, 0, first : first + JB], ACT.Exp)

        def sum_and_root(g):
            n = chunks_of(g) * JB
            nc.tensor.matmul(sums[g][:, 1, :n], same_user[:], e[g][:, :n], start=True, stop=True)
            inv_den[g] = columns.tile([P, GROUP * JB], F32, name="inv_den")
            nc.scalar.activation(inv_den[g][:, :n], sums[g][:, 1, :n], ACT.Abs_reciprocal_sqrt)

        def weights(g):
            n = chunks_of(g) * JB
            a[g] = columns.tile([P, GROUP * JB], F32, name="a")
            nc.vector.tensor_tensor(a[g][:, :n], e[g][:, :n], inv_den[g][:, :n], MULT)

        def spread_weights(k):
            g, first = k // GROUP, (k % GROUP) * JB
            diagonals = staged.tile([P, JB, P], F32, name="diagonals")
            for jb in range(JB):
                nc.scalar.activation(
                    diagonals[:, jb, :], identity[:], ACT.Copy, scale=a[g][:, first + jb : first + jb + 1]
                )
            a_rows[k] = weight_rows.tile([P, CHUNK], F32, name="a_rows")
            nc.tensor.matmul(
                a_rows[k][:], ones[:], diagonals[:].rearrange("p b j -> p (b j)"), start=True, stop=True
            )

        def weigh_and_store(k):
            gp_row = rows.tile([P, GP_COLS], F32, name="gp_row")
            nc.vector.tensor_copy(gp_row[:], a_rows[k][:, V_COLS:])
            per = RB if k + LAG < CHUNKS else 2 * RB
            pieces = [(cb, per) for cb in range(0, CB, per)]
            if k == CHUNKS - 1:
                pieces = pieces[:-1] + [(CB - 2 * RB, RB)] + [(cb, 1) for cb in range(CB - RB, CB)]
            for cb, blocks in pieces:
                weighted = outgoing.tile([P, 2 * RB, CHUNK], F32, name="weighted")
                nc.gpsimd.tensor_tensor(
                    weighted[:, :blocks, V_COLS:],
                    x[k][:, cb : cb + blocks, V_COLS:],
                    gp_row[:].unsqueeze(1).to_broadcast([P, blocks, GP_COLS]),
                    MULT,
                )
                nc.vector.tensor_tensor(
                    weighted[:, :blocks, :V_COLS],
                    x[k][:, cb : cb + blocks, :V_COLS],
                    a_rows[k][:, :V_COLS].unsqueeze(1).to_broadcast([P, blocks, V_COLS]),
                    MULT,
                )
                nc.sync.dma_start(
                    out_blocks[:, cb : cb + blocks, k * CHUNK : (k + 1) * CHUNK], weighted[:, :blocks, :]
                )

        turns = list(range(0, CB, RB))
        for rb in turns:
            spread_targ(0, rb)
        for step in range(CHUNKS + LAG):
            late = step - LAG
            ends_group = 1 <= step <= CHUNKS and (step % GROUP == 0 or step == CHUNKS)
            for rb in turns:
                if step + 1 < CHUNKS:
                    spread_targ(step + 1, rb)
                if 1 <= step <= CHUNKS and rb == turns[0]:
                    score(step - 1)
                if step < CHUNKS:
                    look_up(step, rb)
                if ends_group and rb == turns[1]:
                    sum_and_root((step - 1) // GROUP)
                if ends_group and rb == turns[2]:
                    weights((step - 1) // GROUP)
                if 0 <= late + 1 < CHUNKS and rb == turns[1]:
                    spread_weights(late + 1)
                if late >= 0 and rb == turns[1]:
                    weigh_and_store(late)
